import numpy as np
import ml_dtypes


def mxq(x, axis, fmt="e4m3"):
    dtype, down = {"e4m3": (ml_dtypes.float8_e4m3fn, 7), "e5m2": (ml_dtypes.float8_e5m2, 14)}[fmt]
    v = np.moveaxis(np.asarray(x, np.float32).astype(ml_dtypes.bfloat16).astype(np.float64), axis, -1)
    blocks = v.reshape(v.shape[:-1] + (-1, 32))
    amax = np.abs(blocks).max(-1, keepdims=True)
    byte = np.maximum(np.where(amax > 0, np.frexp(amax)[1] - 1 + 127, 0) - down, 1)
    scale = np.exp2(byte - 127.0)
    codes = (blocks / scale).astype(np.float32).astype(dtype).astype(np.float64)
    return np.moveaxis((codes * scale).reshape(v.shape), -1, axis)


WIDE = False


def mx_kscale(k):
    if not WIDE:
        return np.ones(k)
    levels = np.array([10, -10, 5, -5, 0])
    if k % 512:
        return np.exp2(np.random.permutation(np.resize(levels, k // 32))).repeat(32)
    a = np.empty((k // 512, 16))
    for p in range(k // 512):
        a[p, :8] = np.random.permutation(np.resize(levels, 8))
        for g in range(8):
            far = levels[np.abs(levels - a[p, g]) >= 10]
            a[p, g + 8] = far[np.random.randint(len(far))]
    return np.exp2(a.ravel()).repeat(32)


BF16 = ml_dtypes.bfloat16


def bf(x):
    return np.asarray(x, np.float32).astype(BF16)


def f64(x):
    return np.asarray(x).astype(np.float64)


B, C, MID, HH, WW = 4, 256, 1024, 32, 32
N = HH * WW


def setup_inputs():
    s, t = mx_kscale(N), mx_kscale(MID)
    a = np.exp(1.5 * np.random.standard_normal((B, N, N)))
    a = a / a.sum(-1, keepdims=True)
    return {
        "attn": bf(a * s),
        "h_x": bf(np.random.standard_normal((B, MID, N)) * 2.0 * t[:, None] / s),
        "v_w": bf(np.random.standard_normal((C, MID)) * 3.0 / np.sqrt(MID) / t),
        "v_b": bf(np.random.standard_normal(C) * 0.3),
        "x": bf(np.random.standard_normal((B, C, HH, WW))),
    }


def reference(attn, h_x, v_w, v_b, x):
    z = mxq(f64(h_x), 2, "e4m3") @ mxq(f64(attn), 2, "e4m3").transpose(0, 2, 1)
    y = (mxq(f64(v_w), 1, "e4m3") @ mxq(z, 1, "e4m3")) + f64(v_b)[None, :, None]
    return y.reshape(B, C, HH, WW) + f64(x)

@@ -1,0 +1,246 @@
+from contextlib import ExitStack
+
+import concourse.mybir as mybir
+from concourse.masks import make_identity
+
+F32 = mybir.dt.float32
+BF16 = mybir.dt.bfloat16
+U32 = mybir.dt.uint32
+U8 = mybir.dt.uint8
+FP8X4 = mybir.dt.float8_e4m3fn_x4
+ADD = mybir.AluOpType.add
+
+B, C, MID, N = 4, 256, 1024, 1024
+P = 128
+PACK = 4
+K_PASS = P * PACK
+PASSES = N // K_PASS
+PAIRS = PACK // 2
+SLAB = 512
+TILES = SLAB // P
+SLABS_PER_BATCH = (N + MID) // SLAB
+ROUNDS_PER_BATCH = (N // SLAB) * (MID // SLAB)
+C_TILES = C // P
+SLABS = B * SLABS_PER_BATCH
+ROUNDS = B * ROUNDS_PER_BATCH
+UNITS = B * (N // SLAB) * C_TILES
+RAW_BUFS = 8
+AHEAD = 2
+
+FLOPS = 2 * B * (MID * N * N + C * MID * N)
+
+
+def tile_soablock_pb_t_kernel(tc, attn, h_x, v_w, v_b, x, out):
+    nc = tc.nc
+    x_rows = x.rearrange("b c h w -> b c (h w)")
+    out_rows = out.rearrange("b c h w -> b c (h w)")
+
+    with ExitStack() as ctx:
+        const = ctx.enter_context(tc.tile_pool(name="const", bufs=1))
+        raw_pool = ctx.enter_context(tc.tile_pool(name="raw", bufs=RAW_BUFS))
+        grouped_pool = ctx.enter_context(tc.tile_pool(name="grouped", bufs=2))
+        slab_pool = ctx.enter_context(tc.tile_pool(name="slab", bufs=SLABS_PER_BATCH))
+        z_pool = ctx.enter_context(tc.tile_pool(name="z", bufs=2))
+        x_pool = ctx.enter_context(tc.tile_pool(name="x", bufs=B))
+        result_pool = ctx.enter_context(tc.tile_pool(name="result", bufs=4))
+        square_pool = ctx.enter_context(tc.psum_pool(name="squares", bufs=4))
+        sum_pool = ctx.enter_context(tc.psum_pool(name="sums", bufs=4))
+        ctx.enter_context(tc.manual_schedule())
+
+        raw_of = {}
+        grouped_of = {}
+        codes_of = {}
+        x_of = {}
+        z_grouped_of = {}
+        z_codes_of = {}
+        y_of = {}
+
+        def slab_rows(s):
+            b, place = divmod(s, SLABS_PER_BATCH)
+            if place == 0:
+                return attn[b, 0:SLAB, :].rearrange("(r p) m -> p r m", p=P)
+            if place == 3:
+                return attn[b, SLAB:N, :].rearrange("(r p) m -> p r m", p=P)
+            first = (place - 1) * SLAB
+            return h_x[b, first : first + SLAB, :].rearrange("(p t) m -> p t m", t=TILES)
+
+        def load_slab(s):
+            raw = raw_pool.tile([P, TILES * N], BF16)
+            nc.sync.dma_start(out=raw[:].rearrange("p (r m) -> p r m", r=TILES), in_=slab_rows(s))
+            raw_of[s] = raw
+            b, place = divmod(s, SLABS_PER_BATCH)
+            if place == SLABS_PER_BATCH - 1:
+                residual = x_pool.tile([P, C_TILES, N], BF16)
+                nc.sync.dma_start(out=residual[:], in_=x_rows[b].rearrange("(a p) n -> p a n", p=P))
+                x_of[b] = residual
+
+        def transpose_slab(s):
+            words = raw_of[s][:].bitcast(F32)
+            grouped = grouped_pool.tile([P, TILES * PASSES * P * PACK], BF16, align_bytes=64)
+            grouped_words = grouped[:].bitcast(F32).rearrange(
+                "p (r k c u) -> p r k c u", r=TILES, k=PASSES, u=PAIRS
+            )
+            for r in range(TILES):
+                bank = square_pool.tile([P, PASSES, PAIRS, P], F32, tag="bank")
+                for k in range(PASSES):
+                    for u in range(PAIRS):
+                        first = (r * PASSES + k) * PAIRS * P
+                        nc.tensor.transpose(
+                            out=bank[:, k, u, :],
+                            in_=words[:, first + u : first + PAIRS * P : PAIRS],
+                            identity=ident_f32[:],
+                        )
+                regrouped = bank[:].rearrange("p k u c -> p k c u")
+                if r % 2 == 0:
+                    nc.scalar.copy(out=grouped_words[:, r, :, :, :], in_=regrouped)
+                else:
+                    nc.vector.tensor_copy(out=grouped_words[:, r, :, :, :], in_=regrouped)
+            grouped_of[s] = grouped
+            if s + RAW_BUFS < SLABS:
+                load_slab(s + RAW_BUFS)
+
+        def quantise_slab(s):
+            codes = slab_pool.tile([P, TILES, PASSES, P], U32, align_bytes=64)
+            scales = slab_pool.tile([P, TILES, PASSES, P], U8, align_bytes=64)
+            nc.vector.quantize_mx(
+                out=codes[:].rearrange("p r k c -> p (r k c)").bitcast(FP8X4),
+                scales=scales[:].rearrange("p r k c -> p (r k c)"),
+                in_=grouped_of[s][:],
+            )
+            codes_of[s] = (codes, scales)
+
+        def mix_positions(j):
+            b, place = divmod(j, ROUNDS_PER_BATCH)
+            half, g = divmod(place, MID // SLAB)
+            a_codes, a_scales = codes_of[b * SLABS_PER_BATCH + 3 * half]
+            h_codes, h_scales = codes_of[b * SLABS_PER_BATCH + 1 + g]
+            z_grouped = z_pool.tile([P, TILES, P, PACK], BF16, align_bytes=64)
+            for r in range(TILES):
+                z_bank = sum_pool.tile([P, PACK, P], F32, tag="sums")
+                for t in range(PACK):
+                    for k in range(PASSES):
+                        nc.tensor.matmul_mx(
+                            out=z_bank[:, t, :],
+                            lhsT=h_codes[:, t, k, :].bitcast(FP8X4),
+                            lhsT_scale=h_scales[:, t, k, :],
+                            rhs=a_codes[:, r, k, :].bitcast(FP8X4),
+                            rhs_scale=a_scales[:, r, k, :],
+                            start=(k == 0),
+                            stop=(k == PASSES - 1),
+                        )
+                nc.scalar.copy(out=z_grouped[:, r, :, :], in_=z_bank[:].rearrange("p t n -> p n t"))
+            z_grouped_of[j] = z_grouped
+
+        def quantise_z(j):
+            b, place = divmod(j, ROUNDS_PER_BATCH)
+            half, g = divmod(place, MID // SLAB)
+            if g == 0:
+                z_codes = z_pool.tile([P, PASSES, SLAB], U32, align_bytes=64)
+                z_scales = z_pool.tile([P, PASSES, SLAB], U8, align_bytes=64)
+                z_codes_of[(b, half)] = (z_codes, z_scales)
+            z_codes, z_scales = z_codes_of[(b, half)]
+            nc.vector.quantize_mx(
+                out=z_codes[:, g, :].bitcast(FP8X4),
+                scales=z_scales[:, g, :],
+                in_=z_grouped_of[j][:].rearrange("p r n t -> p (r n t)"),
+            )
+
+        def map_channels(i):
+            b, place = divmod(i, UNITS // B)
+            half, a = divmod(place, C_TILES)
+            z_codes, z_scales = z_codes_of[(b, half)]
+            o_cols = slice(a * P, (a + 1) * P)
+            y_bank = sum_pool.tile([P, SLAB], F32, tag="sums")
+            for g in range(PASSES):
+                nc.tensor.matmul_mx(
+                    out=y_bank[:],
+                    lhsT=w_codes[:, g, o_cols].bitcast(FP8X4),
+                    lhsT_scale=w_scales[:, g, o_cols],
+                    rhs=z_codes[:, g, :].bitcast(FP8X4),
+                    rhs_scale=z_scales[:, g, :],
+                    start=(g == 0),
+                    stop=(g == PASSES - 1),
+                )
+            y_of[i] = y_bank
+
+        def finish(i):
+            b, place = divmod(i, UNITS // B)
+            half, a = divmod(place, C_TILES)
+            n_cols = slice(half * SLAB, (half + 1) * SLAB)
+            result = result_pool.tile([P, SLAB], F32)
+            nc.vector.scalar_tensor_tensor(
+                out=result[:],
+                in0=y_of[i][:],
+                scalar=bias[:, a : a + 1],
+                in1=x_of[b][:, a, n_cols],
+                op0=ADD,
+                op1=ADD,
+            )
+            nc.sync.dma_start(out=out_rows[b, a * P : (a + 1) * P, n_cols], in_=result[:])
+
+        ident_f32 = const.tile([P, P], F32)
+        make_identity(nc, ident_f32[:])
+        ident_bf16 = const.tile([P, P], BF16)
+        make_identity(nc, ident_bf16[:])
+        bias_rows = const.tile([P, P], BF16)
+        nc.vector.memset(bias_rows[:], 0.0)
+
+        load_slab(0)
+        load_slab(1)
+        w_raw = const.tile([P, C_TILES * MID], BF16)
+        nc.sync.dma_start(
+            out=w_raw[:].rearrange("p (a c) -> p a c", a=C_TILES),
+            in_=v_w.rearrange("(a p) c -> p a c", p=P),
+        )
+        nc.sync.dma_start(out=bias_rows[0:C_TILES, :], in_=v_b.rearrange("(a o) -> a o", a=C_TILES))
+        for s in range(2, RAW_BUFS):
+            load_slab(s)
+
+        for s in range(AHEAD):
+            transpose_slab(s)
+            quantise_slab(s)
+
+        w_words = w_raw[:].bitcast(F32).rearrange(
+            "o (a g p u) -> o a g p u", a=C_TILES, g=PASSES, u=PAIRS
+        )
+        w_grouped = const.tile([P, PASSES * C * PACK], BF16, align_bytes=64)
+        w_grouped_words = w_grouped[:].bitcast(F32).rearrange(
+            "p (g a o u) -> p g a o u", g=PASSES, a=C_TILES, u=PAIRS
+        )
+        for a in range(C_TILES):
+            bank = square_pool.tile([P, PASSES, PAIRS, P], F32, tag="bank")
+            for g in range(PASSES):
+                for u in range(PAIRS):
+                    nc.tensor.transpose(
+                        out=bank[:, g, u, :], in_=w_words[:, a, g, :, u], identity=ident_f32[:]
+                    )
+            nc.vector.tensor_copy(
+                out=w_grouped_words[:, :, a, :, :], in_=bank[:].rearrange("p g u o -> p g o u")
+            )
+        w_codes = const.tile([P, PASSES, C], U32, align_bytes=64)
+        w_scales = const.tile([P, PASSES, C], U8, align_bytes=64)
+
+        bias_bank = square_pool.tile([P, P], BF16, tag="bank")
+        nc.tensor.transpose(out=bias_bank[:], in_=bias_rows[:], identity=ident_bf16[:])
+        bias = const.tile([P, C_TILES], F32)
+        nc.vector.tensor_copy(out=bias[:], in_=bias_bank[:, 0:C_TILES])
+
+        nc.vector.quantize_mx(
+            out=w_codes[:].rearrange("p g o -> p (g o)").bitcast(FP8X4),
+            scales=w_scales[:].rearrange("p g o -> p (g o)"),
+            in_=w_grouped[:],
+        )
+
+        for j in range(ROUNDS + 3):
+            if 0 <= j - 3:
+                finish(j - 3)
+            if j + AHEAD < SLABS:
+                transpose_slab(j + AHEAD)
+            if 0 <= j - 1 < ROUNDS:
+                quantise_z(j - 1)
+            if j + AHEAD < SLABS:
+                quantise_slab(j + AHEAD)
+            if j < ROUNDS:
+                mix_positions(j)
+            if 0 <= j - 2 < UNITS:
+                map_channels(j - 2)

@@ -15,6 +15,7 @@ P = 128
 PACK = 4
 K_PASS = P * PACK
 PASSES = N // K_PASS
+GROUP = 8
 PAIRS = PACK // 2
 SLAB = 512
 TILES = SLAB // P
@@ -38,7 +39,8 @@ def tile_soablock_pb_t_kernel(tc, attn, h_x, v_w, v_b, x, out):
     with ExitStack() as ctx:
         const = ctx.enter_context(tc.tile_pool(name="const", bufs=1))
         raw_pool = ctx.enter_context(tc.tile_pool(name="raw", bufs=RAW_BUFS))
-        grouped_pool = ctx.enter_context(tc.tile_pool(name="grouped", bufs=2))
+        sorted_pool = ctx.enter_context(tc.tile_pool(name="sorted", bufs=3))
+        grouped_pool = ctx.enter_context(tc.tile_pool(name="grouped", bufs=3))
         slab_pool = ctx.enter_context(tc.tile_pool(name="slab", bufs=SLABS_PER_BATCH))
         z_pool = ctx.enter_context(tc.tile_pool(name="z", bufs=2))
         x_pool = ctx.enter_context(tc.tile_pool(name="x", bufs=B))
@@ -48,6 +50,7 @@ def tile_soablock_pb_t_kernel(tc, attn, h_x, v_w, v_b, x, out):
         ctx.enter_context(tc.manual_schedule())
 
         raw_of = {}
+        sorted_of = {}
         grouped_of = {}
         codes_of = {}
         x_of = {}
@@ -74,8 +77,18 @@ def tile_soablock_pb_t_kernel(tc, attn, h_x, v_w, v_b, x, out):
                 nc.sync.dma_start(out=residual[:], in_=x_rows[b].rearrange("(a p) n -> p a n", p=P))
                 x_of[b] = residual
 
+        def sort_slab(s):
+            parted = sorted_pool.tile([P, PAIRS, TILES * N // PAIRS], BF16)
+            nc.vector.tensor_copy(
+                out=parted[:].rearrange("p u (y i) -> p u y i", i=2 * GROUP),
+                in_=raw_of[s][:].rearrange("p (y u i) -> p u y i", u=PAIRS, i=2 * GROUP),
+            )
+            sorted_of[s] = parted
+            if s + RAW_BUFS < SLABS:
+                load_slab(s + RAW_BUFS)
+
         def transpose_slab(s):
-            words = raw_of[s][:].bitcast(F32)
+            words = sorted_of[s][:].bitcast(F32)
             grouped = grouped_pool.tile([P, TILES * PASSES * P * PACK], BF16, align_bytes=64)
             grouped_words = grouped[:].bitcast(F32).rearrange(
                 "p (r k c u) -> p r k c u", r=TILES, k=PASSES, u=PAIRS
@@ -84,20 +97,18 @@ def tile_soablock_pb_t_kernel(tc, attn, h_x, v_w, v_b, x, out):
                 bank = square_pool.tile([P, PASSES, PAIRS, P], F32, tag="bank")
                 for k in range(PASSES):
                     for u in range(PAIRS):
-                        first = (r * PASSES + k) * PAIRS * P
+                        first = (r * PASSES + k) * P
                         nc.tensor.transpose(
                             out=bank[:, k, u, :],
-                            in_=words[:, first + u : first + PAIRS * P : PAIRS],
+                            in_=words[:, u, first : first + P],
                             identity=ident_f32[:],
                         )
                 regrouped = bank[:].rearrange("p k u c -> p k c u")
-                if r % 2 == 0:
+                if r != 1:
                     nc.scalar.copy(out=grouped_words[:, r, :, :, :], in_=regrouped)
                 else:
                     nc.vector.tensor_copy(out=grouped_words[:, r, :, :, :], in_=regrouped)
             grouped_of[s] = grouped
-            if s + RAW_BUFS < SLABS:
-                load_slab(s + RAW_BUFS)
 
         def quantise_slab(s):
             codes = slab_pool.tile([P, TILES, PASSES, P], U32, align_bytes=64)
@@ -197,8 +208,10 @@ def tile_soablock_pb_t_kernel(tc, attn, h_x, v_w, v_b, x, out):
             load_slab(s)
 
         for s in range(AHEAD):
+            sort_slab(s)
             transpose_slab(s)
             quantise_slab(s)
+        sort_slab(AHEAD)
 
         w_words = w_raw[:].bitcast(F32).rearrange(
             "o (a g p u) -> o a g p u", a=C_TILES, g=PASSES, u=PAIRS
@@ -238,6 +251,8 @@ def tile_soablock_pb_t_kernel(tc, attn, h_x, v_w, v_b, x, out):
                 transpose_slab(j + AHEAD)
             if 0 <= j - 1 < ROUNDS:
                 quantise_z(j - 1)
+            if j + AHEAD + 1 < SLABS:
+                sort_slab(j + AHEAD + 1)
             if j + AHEAD < SLABS:
                 quantise_slab(j + AHEAD)
             if j < ROUNDS:

@@ -67,9 +67,12 @@ def tile_soablock_pb_t_kernel(tc, attn, h_x, v_w, v_b, x, out):
             first = (place - 1) * SLAB
             return h_x[b, first : first + SLAB, :].rearrange("(p t) m -> p t m", t=TILES)
 
-        def load_slab(s):
+        def load_slab(s, pieces=1):
             raw = raw_pool.tile([P, TILES * N], BF16)
-            nc.sync.dma_start(out=raw[:].rearrange("p (r m) -> p r m", r=TILES), in_=slab_rows(s))
+            raw_rows = raw[:].rearrange("p (r m) -> p r m", r=TILES)
+            step = TILES // pieces
+            for r in range(0, TILES, step):
+                nc.sync.dma_start(out=raw_rows[:, r : r + step, :], in_=slab_rows(s)[:, r : r + step, :])
             raw_of[s] = raw
             b, place = divmod(s, SLABS_PER_BATCH)
             if place == SLABS_PER_BATCH - 1:
@@ -77,23 +80,31 @@ def tile_soablock_pb_t_kernel(tc, attn, h_x, v_w, v_b, x, out):
                 nc.sync.dma_start(out=residual[:], in_=x_rows[b].rearrange("(a p) n -> p a n", p=P))
                 x_of[b] = residual
 
-        def sort_slab(s):
-            parted = sorted_pool.tile([P, PAIRS, TILES * N // PAIRS], BF16)
+        def sort_rows(s, first, count):
+            if first == 0:
+                sorted_of[s] = sorted_pool.tile([P, PAIRS, TILES * N // PAIRS], BF16, name="parted")
+            half = N // PAIRS
             nc.vector.tensor_copy(
-                out=parted[:].rearrange("p u (y i) -> p u y i", i=2 * GROUP),
-                in_=raw_of[s][:].rearrange("p (y u i) -> p u y i", u=PAIRS, i=2 * GROUP),
+                out=sorted_of[s][:, :, first * half : (first + count) * half].rearrange(
+                    "p u (y i) -> p u y i", i=2 * GROUP
+                ),
+                in_=raw_of[s][:, first * N : (first + count) * N].rearrange(
+                    "p (y u i) -> p u y i", u=PAIRS, i=2 * GROUP
+                ),
             )
-            sorted_of[s] = parted
-            if s + RAW_BUFS < SLABS:
+            if first + count == TILES and s + RAW_BUFS < SLABS:
                 load_slab(s + RAW_BUFS)
 
-        def transpose_slab(s):
+        def transpose_rows(s, rows, on_vector):
             words = sorted_of[s][:].bitcast(F32)
-            grouped = grouped_pool.tile([P, TILES * PASSES * P * PACK], BF16, align_bytes=64)
-            grouped_words = grouped[:].bitcast(F32).rearrange(
+            if s not in grouped_of:
+                grouped_of[s] = grouped_pool.tile(
+                    [P, TILES * PASSES * P * PACK], BF16, name="grouped", align_bytes=64
+                )
+            grouped_words = grouped_of[s][:].bitcast(F32).rearrange(
                 "p (r k c u) -> p r k c u", r=TILES, k=PASSES, u=PAIRS
             )
-            for r in range(TILES):
+            for r in rows:
                 bank = square_pool.tile([P, PASSES, PAIRS, P], F32, tag="bank")
                 for k in range(PASSES):
                     for u in range(PAIRS):
@@ -104,21 +115,24 @@ def tile_soablock_pb_t_kernel(tc, attn, h_x, v_w, v_b, x, out):
                             identity=ident_f32[:],
                         )
                 regrouped = bank[:].rearrange("p k u c -> p k c u")
-                if r != 1:
-                    nc.scalar.copy(out=grouped_words[:, r, :, :, :], in_=regrouped)
-                else:
+                if r in on_vector:
                     nc.vector.tensor_copy(out=grouped_words[:, r, :, :, :], in_=regrouped)
-            grouped_of[s] = grouped
+                else:
+                    nc.scalar.copy(out=grouped_words[:, r, :, :, :], in_=regrouped)
 
-        def quantise_slab(s):
-            codes = slab_pool.tile([P, TILES, PASSES, P], U32, align_bytes=64)
-            scales = slab_pool.tile([P, TILES, PASSES, P], U8, align_bytes=64)
+        def quantise_rows(s, first, count):
+            if first == 0:
+                codes = slab_pool.tile([P, TILES, PASSES, P], U32, align_bytes=64)
+                scales = slab_pool.tile([P, TILES, PASSES, P], U8, align_bytes=64)
+                codes_of[s] = (codes, scales)
+            codes, scales = codes_of[s]
+            rows = slice(first, first + count)
+            values = PASSES * P * PACK
             nc.vector.quantize_mx(
-                out=codes[:].rearrange("p r k c -> p (r k c)").bitcast(FP8X4),
-                scales=scales[:].rearrange("p r k c -> p (r k c)"),
-                in_=grouped_of[s][:],
+                out=codes[:, rows, :, :].rearrange("p r k c -> p (r k c)").bitcast(FP8X4),
+                scales=scales[:, rows, :, :].rearrange("p r k c -> p (r k c)"),
+                in_=grouped_of[s][:, first * values : (first + count) * values],
             )
-            codes_of[s] = (codes, scales)
 
         def mix_positions(j):
             b, place = divmod(j, ROUNDS_PER_BATCH)
@@ -196,65 +210,75 @@ def tile_soablock_pb_t_kernel(tc, attn, h_x, v_w, v_b, x, out):
         bias_rows = const.tile([P, P], BF16)
         nc.vector.memset(bias_rows[:], 0.0)
 
-        load_slab(0)
-        load_slab(1)
+        for s in range(AHEAD):
+            load_slab(s, pieces=TILES)
+        load_slab(2)
         w_raw = const.tile([P, C_TILES * MID], BF16)
         nc.sync.dma_start(
             out=w_raw[:].rearrange("p (a c) -> p a c", a=C_TILES),
             in_=v_w.rearrange("(a p) c -> p a c", p=P),
         )
         nc.sync.dma_start(out=bias_rows[0:C_TILES, :], in_=v_b.rearrange("(a o) -> a o", a=C_TILES))
-        for s in range(2, RAW_BUFS):
+        for s in range(AHEAD + 1, RAW_BUFS):
             load_slab(s)
 
-        for s in range(AHEAD):
-            sort_slab(s)
-            transpose_slab(s)
-            quantise_slab(s)
-        sort_slab(AHEAD)
+        lag = 2
+        for i in range(AHEAD * TILES + lag):
+            if i < AHEAD * TILES:
+                s, r = divmod(i, TILES)
+                sort_rows(s, r, 1)
+                transpose_rows(s, (r,), on_vector=())
+            if i >= lag and (i - lag) % 2 == 1:
+                s, r = divmod(i - lag, TILES)
+                quantise_rows(s, r - 1, 2)
+        sort_rows(AHEAD, 0, TILES)
 
-        w_words = w_raw[:].bitcast(F32).rearrange(
-            "o (a g p u) -> o a g p u", a=C_TILES, g=PASSES, u=PAIRS
-        )
-        w_grouped = const.tile([P, PASSES * C * PACK], BF16, align_bytes=64)
-        w_grouped_words = w_grouped[:].bitcast(F32).rearrange(
-            "p (g a o u) -> p g a o u", g=PASSES, a=C_TILES, u=PAIRS
-        )
-        for a in range(C_TILES):
-            bank = square_pool.tile([P, PASSES, PAIRS, P], F32, tag="bank")
-            for g in range(PASSES):
-                for u in range(PAIRS):
-                    nc.tensor.transpose(
-                        out=bank[:, g, u, :], in_=w_words[:, a, g, :, u], identity=ident_f32[:]
-                    )
-            nc.vector.tensor_copy(
-                out=w_grouped_words[:, :, a, :, :], in_=bank[:].rearrange("p g u o -> p g o u")
-            )
         w_codes = const.tile([P, PASSES, C], U32, align_bytes=64)
         w_scales = const.tile([P, PASSES, C], U8, align_bytes=64)
-
-        bias_bank = square_pool.tile([P, P], BF16, tag="bank")
-        nc.tensor.transpose(out=bias_bank[:], in_=bias_rows[:], identity=ident_bf16[:])
         bias = const.tile([P, C_TILES], F32)
-        nc.vector.tensor_copy(out=bias[:], in_=bias_bank[:, 0:C_TILES])
 
-        nc.vector.quantize_mx(
-            out=w_codes[:].rearrange("p g o -> p (g o)").bitcast(FP8X4),
-            scales=w_scales[:].rearrange("p g o -> p (g o)"),
-            in_=w_grouped[:],
-        )
+        def prepare_weights():
+            w_words = w_raw[:].bitcast(F32).rearrange(
+                "o (a g p u) -> o a g p u", a=C_TILES, g=PASSES, u=PAIRS
+            )
+            w_grouped = const.tile([P, PASSES * C * PACK], BF16, align_bytes=64)
+            w_grouped_words = w_grouped[:].bitcast(F32).rearrange(
+                "p (g a o u) -> p g a o u", g=PASSES, a=C_TILES, u=PAIRS
+            )
+            for a in range(C_TILES):
+                bank = square_pool.tile([P, PASSES, PAIRS, P], F32, tag="bank")
+                for g in range(PASSES):
+                    for u in range(PAIRS):
+                        nc.tensor.transpose(
+                            out=bank[:, g, u, :], in_=w_words[:, a, g, :, u], identity=ident_f32[:]
+                        )
+                nc.vector.tensor_copy(
+                    out=w_grouped_words[:, :, a, :, :], in_=bank[:].rearrange("p g u o -> p g o u")
+                )
+
+            bias_bank = square_pool.tile([P, P], BF16, tag="bank")
+            nc.tensor.transpose(out=bias_bank[:], in_=bias_rows[:], identity=ident_bf16[:])
+            nc.vector.tensor_copy(out=bias[:], in_=bias_bank[:, 0:C_TILES])
+
+            nc.vector.quantize_mx(
+                out=w_codes[:].rearrange("p g o -> p (g o)").bitcast(FP8X4),
+                scales=w_scales[:].rearrange("p g o -> p (g o)"),
+                in_=w_grouped[:],
+            )
 
         for j in range(ROUNDS + 3):
             if 0 <= j - 3:
                 finish(j - 3)
             if j + AHEAD < SLABS:
-                transpose_slab(j + AHEAD)
+                transpose_rows(j + AHEAD, range(TILES), on_vector=(1,))
             if 0 <= j - 1 < ROUNDS:
                 quantise_z(j - 1)
             if j + AHEAD + 1 < SLABS:
-                sort_slab(j + AHEAD + 1)
+                sort_rows(j + AHEAD + 1, 0, TILES)
             if j + AHEAD < SLABS:
-                quantise_slab(j + AHEAD)
+                quantise_rows(j + AHEAD, 0, TILES)
+            if j == 1:
+                prepare_weights()
             if j < ROUNDS:
                 mix_positions(j)
             if 0 <= j - 2 < UNITS:

@@ -39,7 +39,7 @@ def tile_soablock_pb_t_kernel(tc, attn, h_x, v_w, v_b, x, out):
     with ExitStack() as ctx:
         const = ctx.enter_context(tc.tile_pool(name="const", bufs=1))
         raw_pool = ctx.enter_context(tc.tile_pool(name="raw", bufs=RAW_BUFS))
-        sorted_pool = ctx.enter_context(tc.tile_pool(name="sorted", bufs=3))
+        sorted_pool = ctx.enter_context(tc.tile_pool(name="sorted", bufs=4))
         grouped_pool = ctx.enter_context(tc.tile_pool(name="grouped", bufs=3))
         slab_pool = ctx.enter_context(tc.tile_pool(name="slab", bufs=SLABS_PER_BATCH))
         z_pool = ctx.enter_context(tc.tile_pool(name="z", bufs=2))
@@ -81,13 +81,12 @@ def tile_soablock_pb_t_kernel(tc, attn, h_x, v_w, v_b, x, out):
                 x_of[b] = residual
 
         def sort_rows(s, first, count):
-            if first == 0:
-                sorted_of[s] = sorted_pool.tile([P, PAIRS, TILES * N // PAIRS], BF16, name="parted")
-            half = N // PAIRS
+            parted = sorted_pool.tile([P, PAIRS, count * N // PAIRS], BF16, tag="parted%d" % count)
+            for r in range(count):
+                words = slice(r * PASSES * P, (r + 1) * PASSES * P)
+                sorted_of[(s, first + r)] = parted[:].bitcast(F32)[:, :, words]
             nc.vector.tensor_copy(
-                out=sorted_of[s][:, :, first * half : (first + count) * half].rearrange(
-                    "p u (y i) -> p u y i", i=2 * GROUP
-                ),
+                out=parted[:].rearrange("p u (y i) -> p u y i", i=2 * GROUP),
                 in_=raw_of[s][:, first * N : (first + count) * N].rearrange(
                     "p (y u i) -> p u y i", u=PAIRS, i=2 * GROUP
                 ),
@@ -96,7 +95,6 @@ def tile_soablock_pb_t_kernel(tc, attn, h_x, v_w, v_b, x, out):
                 load_slab(s + RAW_BUFS)
 
         def transpose_rows(s, rows, on_vector):
-            words = sorted_of[s][:].bitcast(F32)
             if s not in grouped_of:
                 grouped_of[s] = grouped_pool.tile(
                     [P, TILES * PASSES * P * PACK], BF16, name="grouped", align_bytes=64
@@ -106,12 +104,12 @@ def tile_soablock_pb_t_kernel(tc, attn, h_x, v_w, v_b, x, out):
             )
             for r in rows:
                 bank = square_pool.tile([P, PASSES, PAIRS, P], F32, tag="bank")
+                words = sorted_of[(s, r)]
                 for k in range(PASSES):
                     for u in range(PAIRS):
-                        first = (r * PASSES + k) * P
                         nc.tensor.transpose(
                             out=bank[:, k, u, :],
-                            in_=words[:, u, first : first + P],
+                            in_=words[:, u, k * P : (k + 1) * P],
                             identity=ident_f32[:],
                         )
                 regrouped = bank[:].rearrange("p k u c -> p k c u")
@@ -222,16 +220,17 @@ def tile_soablock_pb_t_kernel(tc, attn, h_x, v_w, v_b, x, out):
         for s in range(AHEAD + 1, RAW_BUFS):
             load_slab(s)
 
-        lag = 2
+        lag = 4
         for i in range(AHEAD * TILES + lag):
             if i < AHEAD * TILES:
                 s, r = divmod(i, TILES)
                 sort_rows(s, r, 1)
                 transpose_rows(s, (r,), on_vector=())
+            if i == AHEAD * TILES + lag - 1:
+                sort_rows(AHEAD, 0, TILES)
             if i >= lag and (i - lag) % 2 == 1:
                 s, r = divmod(i - lag, TILES)
                 quantise_rows(s, r - 1, 2)
-        sort_rows(AHEAD, 0, TILES)
 
         w_codes = const.tile([P, PASSES, C], U32, align_bytes=64)
         w_scales = const.tile([P, PASSES, C], U8, align_bytes=64)

@@ -24,9 +24,9 @@ ROUNDS_PER_BATCH = (N // SLAB) * (MID // SLAB)
 C_TILES = C // P
 SLABS = B * SLABS_PER_BATCH
 ROUNDS = B * ROUNDS_PER_BATCH
-UNITS = B * (N // SLAB) * C_TILES
+HALVES = B * (N // SLAB)
 RAW_BUFS = 8
-AHEAD = 2
+PSUM_BANKS = 8
 
 FLOPS = 2 * B * (MID * N * N + C * MID * N)
 
@@ -41,12 +41,11 @@ def tile_soablock_pb_t_kernel(tc, attn, h_x, v_w, v_b, x, out):
         raw_pool = ctx.enter_context(tc.tile_pool(name="raw", bufs=RAW_BUFS))
         sorted_pool = ctx.enter_context(tc.tile_pool(name="sorted", bufs=4))
         grouped_pool = ctx.enter_context(tc.tile_pool(name="grouped", bufs=3))
-        slab_pool = ctx.enter_context(tc.tile_pool(name="slab", bufs=SLABS_PER_BATCH))
+        slab_pool = ctx.enter_context(tc.tile_pool(name="slab", bufs=SLABS_PER_BATCH + 1))
         z_pool = ctx.enter_context(tc.tile_pool(name="z", bufs=2))
         x_pool = ctx.enter_context(tc.tile_pool(name="x", bufs=B))
         result_pool = ctx.enter_context(tc.tile_pool(name="result", bufs=4))
-        square_pool = ctx.enter_context(tc.psum_pool(name="squares", bufs=4))
-        sum_pool = ctx.enter_context(tc.psum_pool(name="sums", bufs=4))
+        bank_pool = ctx.enter_context(tc.psum_pool(name="banks", bufs=PSUM_BANKS))
         ctx.enter_context(tc.manual_schedule())
 
         raw_of = {}
@@ -56,16 +55,13 @@ def tile_soablock_pb_t_kernel(tc, attn, h_x, v_w, v_b, x, out):
         x_of = {}
         z_grouped_of = {}
         z_codes_of = {}
-        y_of = {}
 
         def slab_rows(s):
             b, place = divmod(s, SLABS_PER_BATCH)
-            if place == 0:
-                return attn[b, 0:SLAB, :].rearrange("(r p) m -> p r m", p=P)
-            if place == 3:
-                return attn[b, SLAB:N, :].rearrange("(r p) m -> p r m", p=P)
-            first = (place - 1) * SLAB
-            return h_x[b, first : first + SLAB, :].rearrange("(p t) m -> p t m", t=TILES)
+            first = (place // 2) * SLAB
+            if place % 2 == 0:
+                return h_x[b, first : first + SLAB, :].rearrange("(p t) m -> p t m", t=TILES)
+            return attn[b, first : first + SLAB, :].rearrange("(r p) m -> p r m", p=P)
 
         def load_slab(s, pieces=1):
             raw = raw_pool.tile([P, TILES * N], BF16)
@@ -74,11 +70,14 @@ def tile_soablock_pb_t_kernel(tc, attn, h_x, v_w, v_b, x, out):
             for r in range(0, TILES, step):
                 nc.sync.dma_start(out=raw_rows[:, r : r + step, :], in_=slab_rows(s)[:, r : r + step, :])
             raw_of[s] = raw
-            b, place = divmod(s, SLABS_PER_BATCH)
-            if place == SLABS_PER_BATCH - 1:
-                residual = x_pool.tile([P, C_TILES, N], BF16)
-                nc.sync.dma_start(out=residual[:], in_=x_rows[b].rearrange("(a p) n -> p a n", p=P))
-                x_of[b] = residual
+            b, place = divmod(s - 1, SLABS_PER_BATCH)
+            if (place == 0 and b > 0) or s == SLABS - 1:
+                load_residual(b - 1 if place == 0 else b)
+
+        def load_residual(b):
+            residual = x_pool.tile([P, C_TILES, N], BF16)
+            nc.sync.dma_start(out=residual[:], in_=x_rows[b].rearrange("(a p) n -> p a n", p=P))
+            x_of[b] = residual
 
         def sort_rows(s, first, count):
             parted = sorted_pool.tile([P, PAIRS, count * N // PAIRS], BF16, tag="parted%d" % count)
@@ -103,7 +102,7 @@ def tile_soablock_pb_t_kernel(tc, attn, h_x, v_w, v_b, x, out):
                 "p (r k c u) -> p r k c u", r=TILES, k=PASSES, u=PAIRS
             )
             for r in rows:
-                bank = square_pool.tile([P, PASSES, PAIRS, P], F32, tag="bank")
+                bank = bank_pool.tile([P, PASSES, PAIRS, P], F32, tag="bank")
                 words = sorted_of[(s, r)]
                 for k in range(PASSES):
                     for u in range(PAIRS):
@@ -132,14 +131,14 @@ def tile_soablock_pb_t_kernel(tc, attn, h_x, v_w, v_b, x, out):
                 in_=grouped_of[s][:, first * values : (first + count) * values],
             )
 
-        def mix_positions(j):
-            b, place = divmod(j, ROUNDS_PER_BATCH)
-            half, g = divmod(place, MID // SLAB)
-            a_codes, a_scales = codes_of[b * SLABS_PER_BATCH + 3 * half]
-            h_codes, h_scales = codes_of[b * SLABS_PER_BATCH + 1 + g]
+        def mix_positions(j, on_vector=()):
+            half, g = divmod(j, MID // SLAB)
+            b, place = divmod(half, N // SLAB)
+            h_codes, h_scales = codes_of[b * SLABS_PER_BATCH + 2 * g]
+            a_codes, a_scales = codes_of[b * SLABS_PER_BATCH + 2 * place + 1]
             z_grouped = z_pool.tile([P, TILES, P, PACK], BF16, align_bytes=64)
             for r in range(TILES):
-                z_bank = sum_pool.tile([P, PACK, P], F32, tag="sums")
+                z_bank = bank_pool.tile([P, PACK, P], F32, tag="bank")
                 for t in range(PACK):
                     for k in range(PASSES):
                         nc.tensor.matmul_mx(
@@ -151,49 +150,50 @@ def tile_soablock_pb_t_kernel(tc, attn, h_x, v_w, v_b, x, out):
                             start=(k == 0),
                             stop=(k == PASSES - 1),
                         )
-                nc.scalar.copy(out=z_grouped[:, r, :, :], in_=z_bank[:].rearrange("p t n -> p n t"))
+                interleaved = z_bank[:].rearrange("p t n -> p n t")
+                if r in on_vector:
+                    nc.vector.tensor_copy(out=z_grouped[:, r, :, :], in_=interleaved)
+                else:
+                    nc.scalar.copy(out=z_grouped[:, r, :, :], in_=interleaved)
             z_grouped_of[j] = z_grouped
 
-        def quantise_z(j):
-            b, place = divmod(j, ROUNDS_PER_BATCH)
-            half, g = divmod(place, MID // SLAB)
-            if g == 0:
+        def quantise_z(j, first=0, count=TILES):
+            half, g = divmod(j, MID // SLAB)
+            if g == 0 and first == 0:
                 z_codes = z_pool.tile([P, PASSES, SLAB], U32, align_bytes=64)
                 z_scales = z_pool.tile([P, PASSES, SLAB], U8, align_bytes=64)
-                z_codes_of[(b, half)] = (z_codes, z_scales)
-            z_codes, z_scales = z_codes_of[(b, half)]
+                z_codes_of[half] = (z_codes, z_scales)
+            z_codes, z_scales = z_codes_of[half]
+            cols = slice(first * P, (first + count) * P)
             nc.vector.quantize_mx(
-                out=z_codes[:, g, :].bitcast(FP8X4),
-                scales=z_scales[:, g, :],
-                in_=z_grouped_of[j][:].rearrange("p r n t -> p (r n t)"),
+                out=z_codes[:, g, cols].bitcast(FP8X4),
+                scales=z_scales[:, g, cols],
+                in_=z_grouped_of[j][:, first : first + count, :, :].rearrange("p r n t -> p (r n t)"),
             )
 
-        def map_channels(i):
-            b, place = divmod(i, UNITS // B)
-            half, a = divmod(place, C_TILES)
-            z_codes, z_scales = z_codes_of[(b, half)]
+        def map_channels(half, a, cols):
+            z_codes, z_scales = z_codes_of[half]
             o_cols = slice(a * P, (a + 1) * P)
-            y_bank = sum_pool.tile([P, SLAB], F32, tag="sums")
+            y_bank = bank_pool.tile([P, cols.stop - cols.start], F32, tag="bank")
             for g in range(PASSES):
                 nc.tensor.matmul_mx(
                     out=y_bank[:],
                     lhsT=w_codes[:, g, o_cols].bitcast(FP8X4),
                     lhsT_scale=w_scales[:, g, o_cols],
-                    rhs=z_codes[:, g, :].bitcast(FP8X4),
-                    rhs_scale=z_scales[:, g, :],
+                    rhs=z_codes[:, g, cols].bitcast(FP8X4),
+                    rhs_scale=z_scales[:, g, cols],
                     start=(g == 0),
                     stop=(g == PASSES - 1),
                 )
-            y_of[i] = y_bank
+            return y_bank
 
-        def finish(i):
-            b, place = divmod(i, UNITS // B)
-            half, a = divmod(place, C_TILES)
-            n_cols = slice(half * SLAB, (half + 1) * SLAB)
-            result = result_pool.tile([P, SLAB], F32)
+        def finish(half, a, cols, y_bank):
+            b, place = divmod(half, N // SLAB)
+            n_cols = slice(place * SLAB + cols.start, place * SLAB + cols.stop)
+            result = result_pool.tile([P, cols.stop - cols.start], F32)
             nc.vector.scalar_tensor_tensor(
                 out=result[:],
-                in0=y_of[i][:],
+                in0=y_bank[:],
                 scalar=bias[:, a : a + 1],
                 in1=x_of[b][:, a, n_cols],
                 op0=ADD,
@@ -208,29 +208,18 @@ def tile_soablock_pb_t_kernel(tc, attn, h_x, v_w, v_b, x, out):
         bias_rows = const.tile([P, P], BF16)
         nc.vector.memset(bias_rows[:], 0.0)
 
-        for s in range(AHEAD):
+        for s in range(2):
             load_slab(s, pieces=TILES)
         load_slab(2)
+        load_slab(3)
         w_raw = const.tile([P, C_TILES * MID], BF16)
         nc.sync.dma_start(
             out=w_raw[:].rearrange("p (a c) -> p a c", a=C_TILES),
             in_=v_w.rearrange("(a p) c -> p a c", p=P),
         )
         nc.sync.dma_start(out=bias_rows[0:C_TILES, :], in_=v_b.rearrange("(a o) -> a o", a=C_TILES))
-        for s in range(AHEAD + 1, RAW_BUFS):
+        for s in range(4, RAW_BUFS):
             load_slab(s)
-
-        lag = 4
-        for i in range(AHEAD * TILES + lag):
-            if i < AHEAD * TILES:
-                s, r = divmod(i, TILES)
-                sort_rows(s, r, 1)
-                transpose_rows(s, (r,), on_vector=())
-            if i == AHEAD * TILES + lag - 1:
-                sort_rows(AHEAD, 0, TILES)
-            if i >= lag and (i - lag) % 2 == 1:
-                s, r = divmod(i - lag, TILES)
-                quantise_rows(s, r - 1, 2)
 
         w_codes = const.tile([P, PASSES, C], U32, align_bytes=64)
         w_scales = const.tile([P, PASSES, C], U8, align_bytes=64)
@@ -245,7 +234,7 @@ def tile_soablock_pb_t_kernel(tc, attn, h_x, v_w, v_b, x, out):
                 "p (g a o u) -> p g a o u", g=PASSES, a=C_TILES, u=PAIRS
             )
             for a in range(C_TILES):
-                bank = square_pool.tile([P, PASSES, PAIRS, P], F32, tag="bank")
+                bank = bank_pool.tile([P, PASSES, PAIRS, P], F32, tag="bank")
                 for g in range(PASSES):
                     for u in range(PAIRS):
                         nc.tensor.transpose(
@@ -255,7 +244,7 @@ def tile_soablock_pb_t_kernel(tc, attn, h_x, v_w, v_b, x, out):
                     out=w_grouped_words[:, :, a, :, :], in_=bank[:].rearrange("p g u o -> p g o u")
                 )
 
-            bias_bank = square_pool.tile([P, P], BF16, tag="bank")
+            bias_bank = bank_pool.tile([P, P], BF16, tag="bank")
             nc.tensor.transpose(out=bias_bank[:], in_=bias_rows[:], identity=ident_bf16[:])
             nc.vector.tensor_copy(out=bias[:], in_=bias_bank[:, 0:C_TILES])
 
@@ -265,20 +254,60 @@ def tile_soablock_pb_t_kernel(tc, attn, h_x, v_w, v_b, x, out):
                 in_=w_grouped[:],
             )
 
-        for j in range(ROUNDS + 3):
-            if 0 <= j - 3:
-                finish(j - 3)
-            if j + AHEAD < SLABS:
-                transpose_rows(j + AHEAD, range(TILES), on_vector=(1,))
-            if 0 <= j - 1 < ROUNDS:
-                quantise_z(j - 1)
-            if j + AHEAD + 1 < SLABS:
-                sort_rows(j + AHEAD + 1, 0, TILES)
-            if j + AHEAD < SLABS:
-                quantise_rows(j + AHEAD, 0, TILES)
-            if j == 1:
-                prepare_weights()
-            if j < ROUNDS:
+        for r in range(TILES):
+            sort_rows(0, r, 1)
+            transpose_rows(0, (r,), on_vector=())
+        sort_rows(1, 0, 1)
+        transpose_rows(1, (0,), on_vector=())
+        quantise_rows(0, 0, 2)
+        sort_rows(1, 1, 1)
+        transpose_rows(1, (1,), on_vector=())
+        sort_rows(1, 2, 1)
+        transpose_rows(1, (2,), on_vector=())
+        quantise_rows(0, 2, 2)
+        sort_rows(1, 3, 1)
+        transpose_rows(1, (3,), on_vector=())
+        for r in range(TILES):
+            quantise_rows(1, r, 1)
+        sort_rows(2, 0, TILES)
+
+        all_cols = slice(0, SLAB)
+        for pair in range(HALVES):
+            j = 2 * pair
+            s = j + 2
+            if pair == 0:
                 mix_positions(j)
-            if 0 <= j - 2 < UNITS:
-                map_channels(j - 2)
+                sort_rows(s + 1, 0, TILES)
+                transpose_rows(s, range(TILES), on_vector=(2, 3))
+                transpose_rows(s + 1, range(TILES), on_vector=())
+                quantise_rows(s, 0, TILES)
+                prepare_weights()
+                sort_rows(s + 2, 0, TILES)
+                mix_positions(j + 1)
+                sort_rows(s + 3, 0, TILES)
+                quantise_rows(s + 1, 0, TILES)
+                quantise_z(j)
+                continue
+            quantise_z(j - 1)
+            if s < SLABS:
+                transpose_rows(s, range(TILES), on_vector=(2,))
+                if s + 2 < SLABS:
+                    sort_rows(s + 2, 0, TILES)
+                transpose_rows(s + 1, range(TILES), on_vector=(1,))
+                quantise_rows(s, 0, TILES)
+            mix_positions(j)
+            y_banks = [map_channels(pair - 1, a, all_cols) for a in range(C_TILES)]
+            if s < SLABS:
+                quantise_rows(s + 1, 0, TILES)
+            for a in range(C_TILES):
+                finish(pair - 1, a, all_cols, y_banks[a])
+            mix_positions(j + 1, on_vector=(2,) if pair == HALVES - 1 else ())
+            quantise_z(j)
+            if s + 3 < SLABS:
+                sort_rows(s + 3, 0, TILES)
+
+        for quarter in range(2):
+            quantise_z(ROUNDS - 1, 2 * quarter, 2)
+            cols = slice(quarter * SLAB // 2, (quarter + 1) * SLAB // 2)
+            for a in range(C_TILES):
+                finish(HALVES - 1, a, cols, map_channels(HALVES - 1, a, cols))

@@ -290,10 +290,10 @@ def tile_soablock_pb_t_kernel(tc, attn, h_x, v_w, v_b, x, out):
                 continue
             quantise_z(j - 1)
             if s < SLABS:
-                transpose_rows(s, range(TILES), on_vector=(2,))
+                transpose_rows(s, range(TILES), on_vector=())
                 if s + 2 < SLABS:
                     sort_rows(s + 2, 0, TILES)
-                transpose_rows(s + 1, range(TILES), on_vector=(1,))
+                transpose_rows(s + 1, range(TILES), on_vector=())
                 quantise_rows(s, 0, TILES)
             mix_positions(j)
             y_banks = [map_channels(pair - 1, a, all_cols) for a in range(C_TILES)]

@@ -225,14 +225,13 @@ def tile_soablock_pb_t_kernel(tc, attn, h_x, v_w, v_b, x, out):
         w_scales = const.tile([P, PASSES, C], U8, align_bytes=64)
         bias = const.tile([P, C_TILES], F32)
 
-        def prepare_weights():
+        w_grouped = const.tile([P, PASSES * C * PACK], BF16, align_bytes=64)
+
+        def transpose_weights():
             w_words = w_raw[:].bitcast(F32).rearrange(
                 "o (a g p u) -> o a g p u", a=C_TILES, g=PASSES, u=PAIRS
             )
-            w_grouped = const.tile([P, PASSES * C * PACK], BF16, align_bytes=64)
-            w_grouped_words = w_grouped[:].bitcast(F32).rearrange(
-                "p (g a o u) -> p g a o u", g=PASSES, a=C_TILES, u=PAIRS
-            )
+            w_banks = []
             for a in range(C_TILES):
                 bank = bank_pool.tile([P, PASSES, PAIRS, P], F32, tag="bank")
                 for g in range(PASSES):
@@ -240,14 +239,22 @@ def tile_soablock_pb_t_kernel(tc, attn, h_x, v_w, v_b, x, out):
                         nc.tensor.transpose(
                             out=bank[:, g, u, :], in_=w_words[:, a, g, :, u], identity=ident_f32[:]
                         )
-                nc.vector.tensor_copy(
-                    out=w_grouped_words[:, :, a, :, :], in_=bank[:].rearrange("p g u o -> p g o u")
-                )
-
+                w_banks.append(bank)
             bias_bank = bank_pool.tile([P, P], BF16, tag="bank")
             nc.tensor.transpose(out=bias_bank[:], in_=bias_rows[:], identity=ident_bf16[:])
+            return w_banks, bias_bank
+
+        def regroup_weights(w_banks, bias_bank):
+            w_grouped_words = w_grouped[:].bitcast(F32).rearrange(
+                "p (g a o u) -> p g a o u", g=PASSES, a=C_TILES, u=PAIRS
+            )
+            for a in range(C_TILES):
+                nc.vector.tensor_copy(
+                    out=w_grouped_words[:, :, a, :, :], in_=w_banks[a][:].rearrange("p g u o -> p g o u")
+                )
             nc.vector.tensor_copy(out=bias[:], in_=bias_bank[:, 0:C_TILES])
 
+        def quantise_weights():
             nc.vector.quantize_mx(
                 out=w_codes[:].rearrange("p g o -> p (g o)").bitcast(FP8X4),
                 scales=w_scales[:].rearrange("p g o -> p (g o)"),
@@ -278,22 +285,26 @@ def tile_soablock_pb_t_kernel(tc, attn, h_x, v_w, v_b, x, out):
             if pair == 0:
                 mix_positions(j)
                 sort_rows(s + 1, 0, TILES)
-                transpose_rows(s, range(TILES), on_vector=(2, 3))
+                transpose_rows(s, range(TILES), on_vector=(3,))
                 transpose_rows(s + 1, range(TILES), on_vector=())
                 quantise_rows(s, 0, TILES)
-                prepare_weights()
+                w_banks, bias_bank = transpose_weights()
                 sort_rows(s + 2, 0, TILES)
-                mix_positions(j + 1)
+                regroup_weights(w_banks, bias_bank)
                 sort_rows(s + 3, 0, TILES)
+                mix_positions(j + 1)
                 quantise_rows(s + 1, 0, TILES)
+                quantise_weights()
                 quantise_z(j)
                 continue
             quantise_z(j - 1)
             if s < SLABS:
                 transpose_rows(s, range(TILES), on_vector=())
-                if s + 2 < SLABS:
-                    sort_rows(s + 2, 0, TILES)
-                transpose_rows(s + 1, range(TILES), on_vector=())
+            if s + 2 < SLABS:
+                sort_rows(s + 2, 0, TILES)
+            if s < SLABS:
+                transpose_rows(s + 1, range(TILES), on_vector=(2,))
+            if s < SLABS:
                 quantise_rows(s, 0, TILES)
             mix_positions(j)
             y_banks = [map_channels(pair - 1, a, all_cols) for a in range(C_TILES)]
@@ -302,12 +313,15 @@ def tile_soablock_pb_t_kernel(tc, attn, h_x, v_w, v_b, x, out):
             for a in range(C_TILES):
                 finish(pair - 1, a, all_cols, y_banks[a])
             mix_positions(j + 1, on_vector=(2,) if pair == HALVES - 1 else ())
-            quantise_z(j)
             if s + 3 < SLABS:
                 sort_rows(s + 3, 0, TILES)
+            quantise_z(j)
 
+        quarters = [slice(0, SLAB // 2), slice(SLAB // 2, SLAB)]
+        y_banks = []
         for quarter in range(2):
             quantise_z(ROUNDS - 1, 2 * quarter, 2)
-            cols = slice(quarter * SLAB // 2, (quarter + 1) * SLAB // 2)
-            for a in range(C_TILES):
-                finish(HALVES - 1, a, cols, map_channels(HALVES - 1, a, cols))
+            y_banks += [map_channels(HALVES - 1, a, quarters[quarter]) for a in range(C_TILES)]
+        for i in range(2 * C_TILES):
+            quarter, a = divmod(i, C_TILES)
+            finish(HALVES - 1, a, quarters[quarter], y_banks[i])

@@ -312,10 +312,10 @@ def tile_soablock_pb_t_kernel(tc, attn, h_x, v_w, v_b, x, out):
                 quantise_rows(s + 1, 0, TILES)
             for a in range(C_TILES):
                 finish(pair - 1, a, all_cols, y_banks[a])
-            mix_positions(j + 1, on_vector=(2,) if pair == HALVES - 1 else ())
             if s + 3 < SLABS:
                 sort_rows(s + 3, 0, TILES)
             quantise_z(j)
+            mix_positions(j + 1, on_vector=(2,) if pair == HALVES - 1 else ())
 
         quarters = [slice(0, SLAB // 2), slice(SLAB // 2, SLAB)]
         y_banks = []

@@ -49,7 +49,7 @@ def tile_soablock_pb_t_kernel(tc, attn, h_x, v_w, v_b, x, out):
         ctx.enter_context(tc.manual_schedule())
 
         raw_of = {}
-        sorted_of = {}
+        words_of = {}
         grouped_of = {}
         codes_of = {}
         x_of = {}
@@ -81,16 +81,28 @@ def tile_soablock_pb_t_kernel(tc, attn, h_x, v_w, v_b, x, out):
 
         def sort_rows(s, first, count):
             parted = sorted_pool.tile([P, PAIRS, count * N // PAIRS], BF16, tag="parted%d" % count)
+            rows = raw_of[s][:, first * N : (first + count) * N]
+            if s < SLABS_PER_BATCH:
+                nc.vector.tensor_copy(
+                    out=parted[:].bitcast(F32), in_=rows.bitcast(F32).rearrange("p (y u) -> p u y", u=PAIRS)
+                )
+            else:
+                nc.vector.tensor_copy(
+                    out=parted[:].rearrange("p u (y i) -> p u y i", i=2 * GROUP),
+                    in_=rows.rearrange("p (y u i) -> p u y i", u=PAIRS, i=2 * GROUP),
+                )
+            words = parted[:].bitcast(F32).rearrange("p u (r k q) -> p u r k q", r=count, k=PASSES)
             for r in range(count):
-                words = slice(r * PASSES * P, (r + 1) * PASSES * P)
-                sorted_of[(s, first + r)] = parted[:].bitcast(F32)[:, :, words]
-            nc.vector.tensor_copy(
-                out=parted[:].rearrange("p u (y i) -> p u y i", i=2 * GROUP),
-                in_=raw_of[s][:, first * N : (first + count) * N].rearrange(
-                    "p (y u i) -> p u y i", u=PAIRS, i=2 * GROUP
-                ),
-            )
-            if first + count == TILES and s + RAW_BUFS < SLABS:
+                words_of[(s, first + r)] = words[:, :, r, :, :]
+            if first + count == TILES:
+                load_ahead(s)
+
+        def take_raw_rows(s, r):
+            words = raw_of[s][:, r * N : (r + 1) * N].bitcast(F32)
+            words_of[(s, r)] = words.rearrange("p (k q u) -> p u k q", k=PASSES, u=PAIRS)
+
+        def load_ahead(s):
+            if s + RAW_BUFS < SLABS:
                 load_slab(s + RAW_BUFS)
 
         def transpose_rows(s, rows, on_vector):
@@ -103,12 +115,12 @@ def tile_soablock_pb_t_kernel(tc, attn, h_x, v_w, v_b, x, out):
             )
             for r in rows:
                 bank = bank_pool.tile([P, PASSES, PAIRS, P], F32, tag="bank")
-                words = sorted_of[(s, r)]
+                words = words_of[(s, r)]
                 for k in range(PASSES):
                     for u in range(PAIRS):
                         nc.tensor.transpose(
                             out=bank[:, k, u, :],
-                            in_=words[:, u, k * P : (k + 1) * P],
+                            in_=words[:, u, k, :],
                             identity=ident_f32[:],
                         )
                 regrouped = bank[:].rearrange("p k u c -> p k c u")
@@ -131,13 +143,15 @@ def tile_soablock_pb_t_kernel(tc, attn, h_x, v_w, v_b, x, out):
                 in_=grouped_of[s][:, first * values : (first + count) * values],
             )
 
-        def mix_positions(j, on_vector=()):
+        def mix_positions(j, rows=range(TILES), on_vector=()):
             half, g = divmod(j, MID // SLAB)
             b, place = divmod(half, N // SLAB)
             h_codes, h_scales = codes_of[b * SLABS_PER_BATCH + 2 * g]
             a_codes, a_scales = codes_of[b * SLABS_PER_BATCH + 2 * place + 1]
-            z_grouped = z_pool.tile([P, TILES, P, PACK], BF16, align_bytes=64)
-            for r in range(TILES):
+            if j not in z_grouped_of:
+                z_grouped_of[j] = z_pool.tile([P, TILES, P, PACK], BF16, name="z_grouped", align_bytes=64)
+            z_grouped = z_grouped_of[j]
+            for r in rows:
                 z_bank = bank_pool.tile([P, PACK, P], F32, tag="bank")
                 for t in range(PACK):
                     for k in range(PASSES):
@@ -155,7 +169,6 @@ def tile_soablock_pb_t_kernel(tc, attn, h_x, v_w, v_b, x, out):
                     nc.vector.tensor_copy(out=z_grouped[:, r, :, :], in_=interleaved)
                 else:
                     nc.scalar.copy(out=z_grouped[:, r, :, :], in_=interleaved)
-            z_grouped_of[j] = z_grouped
 
         def quantise_z(j, first=0, count=TILES):
             half, g = divmod(j, MID // SLAB)
@@ -210,7 +223,7 @@ def tile_soablock_pb_t_kernel(tc, attn, h_x, v_w, v_b, x, out):
 
         for s in range(2):
             load_slab(s, pieces=TILES)
-        load_slab(2)
+        load_slab(2, pieces=2)
         load_slab(3)
         w_raw = const.tile([P, C_TILES * MID], BF16)
         nc.sync.dma_start(
@@ -261,42 +274,62 @@ def tile_soablock_pb_t_kernel(tc, attn, h_x, v_w, v_b, x, out):
                 in_=w_grouped[:],
             )
 
-        for r in range(TILES):
-            sort_rows(0, r, 1)
-            transpose_rows(0, (r,), on_vector=())
-        sort_rows(1, 0, 1)
+        all_cols = slice(0, SLAB)
+        for s in range(2):
+            for r in range(TILES):
+                take_raw_rows(s, r)
+        transpose_rows(0, (0,), on_vector=())
+        transpose_rows(0, (1,), on_vector=())
+        transpose_rows(0, (2,), on_vector=())
+        transpose_rows(0, (3,), on_vector=())
         transpose_rows(1, (0,), on_vector=())
         quantise_rows(0, 0, 2)
-        sort_rows(1, 1, 1)
         transpose_rows(1, (1,), on_vector=())
-        sort_rows(1, 2, 1)
         transpose_rows(1, (2,), on_vector=())
         quantise_rows(0, 2, 2)
-        sort_rows(1, 3, 1)
         transpose_rows(1, (3,), on_vector=())
+        quantise_rows(1, 0, 1)
+        quantise_rows(1, 1, 1)
+        quantise_rows(1, 2, 1)
+        quantise_rows(1, 3, 1)
+        for s in range(2):
+            load_ahead(s)
+        mix_positions(0, rows=(0, 1))
         for r in range(TILES):
-            quantise_rows(1, r, 1)
-        sort_rows(2, 0, TILES)
+            take_raw_rows(2, r)
+        transpose_rows(2, (0, 1,), on_vector=(1,))
+        quantise_rows(2, 0, 2)
+        transpose_rows(2, (2, 3,), on_vector=(3,))
+        load_ahead(2)
+        mix_positions(0, rows=(2, 3))
+        quantise_rows(2, 2, 2)
+        sort_rows(3, 0, TILES)
+        mix_positions(1)
+        quantise_z(0)
+        sort_rows(4, 0, TILES)
+        transpose_rows(3, range(TILES), on_vector=(1, 3,))
+        transpose_rows(4, range(TILES), on_vector=())
+        quantise_rows(3, 0, TILES)
+        w_banks, bias_bank = transpose_weights()
+        sort_rows(5, 0, TILES)
+        regroup_weights(w_banks, bias_bank)
+        mix_positions(2)
+        quantise_weights()
+        quantise_z(1)
+        sort_rows(6, 0, TILES)
+        transpose_rows(5, range(TILES), on_vector=())
+        y_banks = [map_channels(0, a, all_cols) for a in range(C_TILES)]
+        quantise_rows(4, 0, TILES)
+        sort_rows(7, 0, TILES)
+        for a in range(C_TILES):
+            finish(0, a, all_cols, y_banks[a])
+        quantise_rows(5, 0, TILES)
+        quantise_z(2)
+        mix_positions(3)
 
-        all_cols = slice(0, SLAB)
-        for pair in range(HALVES):
+        for pair in range(2, HALVES):
             j = 2 * pair
             s = j + 2
-            if pair == 0:
-                mix_positions(j)
-                sort_rows(s + 1, 0, TILES)
-                transpose_rows(s, range(TILES), on_vector=(3,))
-                transpose_rows(s + 1, range(TILES), on_vector=())
-                quantise_rows(s, 0, TILES)
-                w_banks, bias_bank = transpose_weights()
-                sort_rows(s + 2, 0, TILES)
-                regroup_weights(w_banks, bias_bank)
-                sort_rows(s + 3, 0, TILES)
-                mix_positions(j + 1)
-                quantise_rows(s + 1, 0, TILES)
-                quantise_weights()
-                quantise_z(j)
-                continue
             quantise_z(j - 1)
             if s < SLABS:
                 transpose_rows(s, range(TILES), on_vector=())

from contextlib import ExitStack

import concourse.mybir as mybir
from concourse.masks import make_identity

F32 = mybir.dt.float32
BF16 = mybir.dt.bfloat16
U32 = mybir.dt.uint32
U8 = mybir.dt.uint8
FP8X4 = mybir.dt.float8_e4m3fn_x4
ADD = mybir.AluOpType.add

B, C, MID, N = 4, 256, 1024, 1024
P = 128
PACK = 4
K_PASS = P * PACK
PASSES = N // K_PASS
GROUP = 8
PAIRS = PACK // 2
SLAB = 512
TILES = SLAB // P
SLABS_PER_BATCH = (N + MID) // SLAB
ROUNDS_PER_BATCH = (N // SLAB) * (MID // SLAB)
C_TILES = C // P
SLABS = B * SLABS_PER_BATCH
ROUNDS = B * ROUNDS_PER_BATCH
HALVES = B * (N // SLAB)
RAW_BUFS = 8
PSUM_BANKS = 8

FLOPS = 2 * B * (MID * N * N + C * MID * N)


def tile_soablock_pb_t_kernel(tc, attn, h_x, v_w, v_b, x, out):
    nc = tc.nc
    x_rows = x.rearrange("b c h w -> b c (h w)")
    out_rows = out.rearrange("b c h w -> b c (h w)")

    with ExitStack() as ctx:
        const = ctx.enter_context(tc.tile_pool(name="const", bufs=1))
        raw_pool = ctx.enter_context(tc.tile_pool(name="raw", bufs=RAW_BUFS))
        sorted_pool = ctx.enter_context(tc.tile_pool(name="sorted", bufs=4))
        grouped_pool = ctx.enter_context(tc.tile_pool(name="grouped", bufs=3))
        slab_pool = ctx.enter_context(tc.tile_pool(name="slab", bufs=SLABS_PER_BATCH + 1))
        z_pool = ctx.enter_context(tc.tile_pool(name="z", bufs=2))
        x_pool = ctx.enter_context(tc.tile_pool(name="x", bufs=B))
        result_pool = ctx.enter_context(tc.tile_pool(name="result", bufs=4))
        bank_pool = ctx.enter_context(tc.psum_pool(name="banks", bufs=PSUM_BANKS))
        ctx.enter_context(tc.manual_schedule())

        raw_of = {}
        words_of = {}
        grouped_of = {}
        codes_of = {}
        x_of = {}
        z_grouped_of = {}
        z_codes_of = {}

        def slab_rows(s):
            b, place = divmod(s, SLABS_PER_BATCH)
            first = (place // 2) * SLAB
            if place % 2 == 0:
                return h_x[b, first : first + SLAB, :].rearrange("(p t) m -> p t m", t=TILES)
            return attn[b, first : first + SLAB, :].rearrange("(r p) m -> p r m", p=P)

        def load_slab(s, pieces=1):
            raw = raw_pool.tile([P, TILES * N], BF16)
            raw_rows = raw[:].rearrange("p (r m) -> p r m", r=TILES)
            step = TILES // pieces
            for r in range(0, TILES, step):
                nc.sync.dma_start(out=raw_rows[:, r : r + step, :], in_=slab_rows(s)[:, r : r + step, :])
            raw_of[s] = raw
            b, place = divmod(s - 1, SLABS_PER_BATCH)
            if (place == 0 and b > 0) or s == SLABS - 1:
                load_residual(b - 1 if place == 0 else b)

        def load_residual(b):
            residual = x_pool.tile([P, C_TILES, N], BF16)
            nc.sync.dma_start(out=residual[:], in_=x_rows[b].rearrange("(a p) n -> p a n", p=P))
            x_of[b] = residual

        def sort_rows(s, first, count):
            parted = sorted_pool.tile([P, PAIRS, count * N // PAIRS], BF16, tag="parted%d" % count)
            rows = raw_of[s][:, first * N : (first + count) * N]
            if s < SLABS_PER_BATCH:
                nc.vector.tensor_copy(
                    out=parted[:].bitcast(F32), in_=rows.bitcast(F32).rearrange("p (y u) -> p u y", u=PAIRS)
                )
            else:
                nc.vector.tensor_copy(
                    out=parted[:].rearrange("p u (y i) -> p u y i", i=2 * GROUP),
                    in_=rows.rearrange("p (y u i) -> p u y i", u=PAIRS, i=2 * GROUP),
                )
            words = parted[:].bitcast(F32).rearrange("p u (r k q) -> p u r k q", r=count, k=PASSES)
            for r in range(count):
                words_of[(s, first + r)] = words[:, :, r, :, :]
            if first + count == TILES:
                load_ahead(s)

        def take_raw_rows(s, r):
            words = raw_of[s][:, r * N : (r + 1) * N].bitcast(F32)
            words_of[(s, r)] = words.rearrange("p (k q u) -> p u k q", k=PASSES, u=PAIRS)

        def load_ahead(s):
            if s + RAW_BUFS < SLABS:
                load_slab(s + RAW_BUFS)

        def transpose_rows(s, rows, on_vector):
            if s not in grouped_of:
                grouped_of[s] = grouped_pool.tile(
                    [P, TILES * PASSES * P * PACK], BF16, name="grouped", align_bytes=64
                )
            grouped_words = grouped_of[s][:].bitcast(F32).rearrange(
                "p (r k c u) -> p r k c u", r=TILES, k=PASSES, u=PAIRS
            )
            for r in rows:
                bank = bank_pool.tile([P, PASSES, PAIRS, P], F32, tag="bank")
                words = words_of[(s, r)]
                for k in range(PASSES):
                    for u in range(PAIRS):
                        nc.tensor.transpose(
                            out=bank[:, k, u, :],
                            in_=words[:, u, k, :],
                            identity=ident_f32[:],
                        )
                regrouped = bank[:].rearrange("p k u c -> p k c u")
                if r in on_vector:
                    nc.vector.tensor_copy(out=grouped_words[:, r, :, :, :], in_=regrouped)
                else:
                    nc.scalar.copy(out=grouped_words[:, r, :, :, :], in_=regrouped)

        def quantise_rows(s, first, count):
            if first == 0:
                codes = slab_pool.tile([P, TILES, PASSES, P], U32, align_bytes=64)
                scales = slab_pool.tile([P, TILES, PASSES, P], U8, align_bytes=64)
                codes_of[s] = (codes, scales)
            codes, scales = codes_of[s]
            rows = slice(first, first + count)
            values = PASSES * P * PACK
            nc.vector.quantize_mx(
                out=codes[:, rows, :, :].rearrange("p r k c -> p (r k c)").bitcast(FP8X4),
                scales=scales[:, rows, :, :].rearrange("p r k c -> p (r k c)"),
                in_=grouped_of[s][:, first * values : (first + count) * values],
            )

        def mix_positions(j, rows=range(TILES), on_vector=()):
            half, g = divmod(j, MID // SLAB)
            b, place = divmod(half, N // SLAB)
            h_codes, h_scales = codes_of[b * SLABS_PER_BATCH + 2 * g]
            a_codes, a_scales = codes_of[b * SLABS_PER_BATCH + 2 * place + 1]
            if j not in z_grouped_of:
                z_grouped_of[j] = z_pool.tile([P, TILES, P, PACK], BF16, name="z_grouped", align_bytes=64)
            z_grouped = z_grouped_of[j]
            for r in rows:
                z_bank = bank_pool.tile([P, PACK, P], F32, tag="bank")
                for t in range(PACK):
                    for k in range(PASSES):
                        nc.tensor.matmul_mx(
                            out=z_bank[:, t, :],
                            lhsT=h_codes[:, t, k, :].bitcast(FP8X4),
                            lhsT_scale=h_scales[:, t, k, :],
                            rhs=a_codes[:, r, k, :].bitcast(FP8X4),
                            rhs_scale=a_scales[:, r, k, :],
                            start=(k == 0),
                            stop=(k == PASSES - 1),
                        )
                interleaved = z_bank[:].rearrange("p t n -> p n t")
                if r in on_vector:
                    nc.vector.tensor_copy(out=z_grouped[:, r, :, :], in_=interleaved)
                else:
                    nc.scalar.copy(out=z_grouped[:, r, :, :], in_=interleaved)

        def quantise_z(j, first=0, count=TILES):
            half, g = divmod(j, MID // SLAB)
            if g == 0 and first == 0:
                z_codes = z_pool.tile([P, PASSES, SLAB], U32, align_bytes=64)
                z_scales = z_pool.tile([P, PASSES, SLAB], U8, align_bytes=64)
                z_codes_of[half] = (z_codes, z_scales)
            z_codes, z_scales = z_codes_of[half]
            cols = slice(first * P, (first + count) * P)
            nc.vector.quantize_mx(
                out=z_codes[:, g, cols].bitcast(FP8X4),
                scales=z_scales[:, g, cols],
                in_=z_grouped_of[j][:, first : first + count, :, :].rearrange("p r n t -> p (r n t)"),
            )

        def map_channels(half, a, cols):
            z_codes, z_scales = z_codes_of[half]
            o_cols = slice(a * P, (a + 1) * P)
            y_bank = bank_pool.tile([P, cols.stop - cols.start], F32, tag="bank")
            for g in range(PASSES):
                nc.tensor.matmul_mx(
                    out=y_bank[:],
                    lhsT=w_codes[:, g, o_cols].bitcast(FP8X4),
                    lhsT_scale=w_scales[:, g, o_cols],
                    rhs=z_codes[:, g, cols].bitcast(FP8X4),
                    rhs_scale=z_scales[:, g, cols],
                    start=(g == 0),
                    stop=(g == PASSES - 1),
                )
            return y_bank

        def finish(half, a, cols, y_bank):
            b, place = divmod(half, N // SLAB)
            n_cols = slice(place * SLAB + cols.start, place * SLAB + cols.stop)
            result = result_pool.tile([P, cols.stop - cols.start], F32)
            nc.vector.scalar_tensor_tensor(
                out=result[:],
                in0=y_bank[:],
                scalar=bias[:, a : a + 1],
                in1=x_of[b][:, a, n_cols],
                op0=ADD,
                op1=ADD,
            )
            nc.sync.dma_start(out=out_rows[b, a * P : (a + 1) * P, n_cols], in_=result[:])

        ident_f32 = const.tile([P, P], F32)
        make_identity(nc, ident_f32[:])
        ident_bf16 = const.tile([P, P], BF16)
        make_identity(nc, ident_bf16[:])
        bias_rows = const.tile([P, P], BF16)
        nc.vector.memset(bias_rows[:], 0.0)

        for s in range(2):
            load_slab(s, pieces=TILES)
        load_slab(2, pieces=2)
        load_slab(3)
        w_raw = const.tile([P, C_TILES * MID], BF16)
        nc.sync.dma_start(
            out=w_raw[:].rearrange("p (a c) -> p a c", a=C_TILES),
            in_=v_w.rearrange("(a p) c -> p a c", p=P),
        )
        nc.sync.dma_start(out=bias_rows[0:C_TILES, :], in_=v_b.rearrange("(a o) -> a o", a=C_TILES))
        for s in range(4, RAW_BUFS):
            load_slab(s)

        w_codes = const.tile([P, PASSES, C], U32, align_bytes=64)
        w_scales = const.tile([P, PASSES, C], U8, align_bytes=64)
        bias = const.tile([P, C_TILES], F32)

        w_grouped = const.tile([P, PASSES * C * PACK], BF16, align_bytes=64)

        def transpose_weights():
            w_words = w_raw[:].bitcast(F32).rearrange(
                "o (a g p u) -> o a g p u", a=C_TILES, g=PASSES, u=PAIRS
            )
            w_banks = []
            for a in range(C_TILES):
                bank = bank_pool.tile([P, PASSES, PAIRS, P], F32, tag="bank")
                for g in range(PASSES):
                    for u in range(PAIRS):
                        nc.tensor.transpose(
                            out=bank[:, g, u, :], in_=w_words[:, a, g, :, u], identity=ident_f32[:]
                        )
                w_banks.append(bank)
            bias_bank = bank_pool.tile([P, P], BF16, tag="bank")
            nc.tensor.transpose(out=bias_bank[:], in_=bias_rows[:], identity=ident_bf16[:])
            return w_banks, bias_bank

        def regroup_weights(w_banks, bias_bank):
            w_grouped_words = w_grouped[:].bitcast(F32).rearrange(
                "p (g a o u) -> p g a o u", g=PASSES, a=C_TILES, u=PAIRS
            )
            for a in range(C_TILES):
                nc.vector.tensor_copy(
                    out=w_grouped_words[:, :, a, :, :], in_=w_banks[a][:].rearrange("p g u o -> p g o u")
                )
            nc.vector.tensor_copy(out=bias[:], in_=bias_bank[:, 0:C_TILES])

        def quantise_weights():
            nc.vector.quantize_mx(
                out=w_codes[:].rearrange("p g o -> p (g o)").bitcast(FP8X4),
                scales=w_scales[:].rearrange("p g o -> p (g o)"),
                in_=w_grouped[:],
            )

        all_cols = slice(0, SLAB)
        for s in range(2):
            for r in range(TILES):
                take_raw_rows(s, r)
        transpose_rows(0, (0,), on_vector=())
        transpose_rows(0, (1,), on_vector=())
        transpose_rows(0, (2,), on_vector=())
        transpose_rows(0, (3,), on_vector=())
        transpose_rows(1, (0,), on_vector=())
        quantise_rows(0, 0, 2)
        transpose_rows(1, (1,), on_vector=())
        transpose_rows(1, (2,), on_vector=())
        quantise_rows(0, 2, 2)
        transpose_rows(1, (3,), on_vector=())
        quantise_rows(1, 0, 1)
        quantise_rows(1, 1, 1)
        quantise_rows(1, 2, 1)
        quantise_rows(1, 3, 1)
        for s in range(2):
            load_ahead(s)
        mix_positions(0, rows=(0, 1))
        for r in range(TILES):
            take_raw_rows(2, r)
        transpose_rows(2, (0, 1,), on_vector=(1,))
        quantise_rows(2, 0, 2)
        transpose_rows(2, (2, 3,), on_vector=(3,))
        load_ahead(2)
        mix_positions(0, rows=(2, 3))
        quantise_rows(2, 2, 2)
        sort_rows(3, 0, TILES)
        mix_positions(1)
        quantise_z(0)
        sort_rows(4, 0, TILES)
        transpose_rows(3, range(TILES), on_vector=(1, 3,))
        transpose_rows(4, range(TILES), on_vector=())
        quantise_rows(3, 0, TILES)
        w_banks, bias_bank = transpose_weights()
        sort_rows(5, 0, TILES)
        regroup_weights(w_banks, bias_bank)
        mix_positions(2)
        quantise_weights()
        quantise_z(1)
        sort_rows(6, 0, TILES)
        transpose_rows(5, range(TILES), on_vector=())
        y_banks = [map_channels(0, a, all_cols) for a in range(C_TILES)]
        quantise_rows(4, 0, TILES)
        sort_rows(7, 0, TILES)
        for a in range(C_TILES):
            finish(0, a, all_cols, y_banks[a])
        quantise_rows(5, 0, TILES)
        quantise_z(2)
        mix_positions(3)

        for pair in range(2, HALVES):
            j = 2 * pair
            s = j + 2
            quantise_z(j - 1)
            if s < SLABS:
                transpose_rows(s, range(TILES), on_vector=())
            if s + 2 < SLABS:
                sort_rows(s + 2, 0, TILES)
            if s < SLABS:
                transpose_rows(s + 1, range(TILES), on_vector=(2,))
            if s < SLABS:
                quantise_rows(s, 0, TILES)
            mix_positions(j)
            y_banks = [map_channels(pair - 1, a, all_cols) for a in range(C_TILES)]
            if s < SLABS:
                quantise_rows(s + 1, 0, TILES)
            for a in range(C_TILES):
                finish(pair - 1, a, all_cols, y_banks[a])
            if s + 3 < SLABS:
                sort_rows(s + 3, 0, TILES)
            quantise_z(j)
            mix_positions(j + 1, on_vector=(2,) if pair == HALVES - 1 else ())

        quarters = [slice(0, SLAB // 2), slice(SLAB // 2, SLAB)]
        y_banks = []
        for quarter in range(2):
            quantise_z(ROUNDS - 1, 2 * quarter, 2)
            y_banks += [map_channels(HALVES - 1, a, quarters[quarter]) for a in range(C_TILES)]
        for i in range(2 * C_TILES):
            quarter, a = divmod(i, C_TILES)
            finish(HALVES - 1, a, quarters[quarter], y_banks[i])
